import numpy as np
import ml_dtypes


def mxq(x, axis, fmt="e4m3"):
    dtype, down = {"e4m3": (ml_dtypes.float8_e4m3fn, 7), "e5m2": (ml_dtypes.float8_e5m2, 14)}[fmt]
    v = np.moveaxis(np.asarray(x, np.float32).astype(ml_dtypes.bfloat16).astype(np.float64), axis, -1)
    blocks = v.reshape(v.shape[:-1] + (-1, 32))
    amax = np.abs(blocks).max(-1, keepdims=True)
    byte = np.maximum(np.where(amax > 0, np.frexp(amax)[1] - 1 + 127, 0) - down, 1)
    scale = np.exp2(byte - 127.0)
    codes = (blocks / scale).astype(np.float32).astype(dtype).astype(np.float64)
    return np.moveaxis((codes * scale).reshape(v.shape), -1, axis)


WIDE = False


def mx_kscale(k):
    if not WIDE:
        return np.ones(k)
    levels = np.array([10, -10, 5, -5, 0])
    a = np.random.permutation(np.resize(levels, k // 512 * 4)).reshape(k // 512, 4)
    idx = np.arange(k)
    return np.exp2(a[idx // 512, idx % 128 // 32])


BF16 = ml_dtypes.bfloat16


def bf(x):
    return np.asarray(x, np.float32).astype(BF16)


def f64(x):
    return np.asarray(x).astype(np.float64)


B, C, H, W = 4, 512, 64, 32
CH = C // 2
N = H * W
QS = 1.35 * CH ** -0.25


def pool2(t):
    r = t.reshape(B, -1, H // 2, 2, W // 2, 2)
    return r.max(axis=(3, 5)) + r.mean(axis=(3, 5))


def setup_inputs():
    s = mx_kscale(C)
    return {"x": bf(np.random.standard_normal((B, C, H, W)) * s[None, :, None, None]),
            "W1": bf(np.random.standard_normal((CH, C)) * QS / np.sqrt(C) / s),
            "W2": bf(np.random.standard_normal((CH, C)) * QS / np.sqrt(C) / s)}


def reference(x, W1, W2):
    xq = mxq(f64(x).reshape(B, C, N), 1, "e4m3")
    c1 = mxq(f64(W1), 1, "e4m3") @ xq
    c2 = mxq(f64(W2), 1, "e4m3") @ xq
    return pool2(c1.reshape(B, CH, H, W)), c2.reshape(B, CH, H, W)

@@ -1,0 +1,179 @@
+from contextlib import ExitStack
+
+import concourse.mybir as mybir
+from concourse.masks import make_identity
+
+FLOPS = 2 * 512 * 512 * 8192
+
+F32 = mybir.dt.float32
+BF16 = mybir.dt.bfloat16
+U32 = mybir.dt.uint32
+U8 = mybir.dt.uint8
+FP8X4 = mybir.dt.float8_e4m3fn_x4
+ALU = mybir.AluOpType
+AXIS = mybir.AxisListType
+
+P = 128
+CHUNK = 512
+N_CHUNKS = 16
+UNITS = [(0, 0, 1), (0, 1, 1), (0, 2, 2), (1, 0, 4), (2, 0, 4), (3, 0, 4)]
+
+
+def tile_selfspatialattentionmodule_pa_t_kernel(tc, x, W1, W2, out_0, out_1):
+    nc = tc.nc
+    with ExitStack() as ctx:
+        const = ctx.enter_context(tc.tile_pool(name="const", bufs=1))
+        xpool = ctx.enter_context(tc.tile_pool(name="xpool", bufs=1))
+        gpool = ctx.enter_context(tc.tile_pool(name="gpool", bufs=4))
+        qpool = ctx.enter_context(tc.tile_pool(name="qpool", bufs=4))
+        opool = ctx.enter_context(tc.tile_pool(name="opool", bufs=2))
+        psum = ctx.enter_context(tc.psum_pool(name="psum", bufs=2))
+
+        w_sb = const.tile([P, 4 * 512], BF16, name="w_sb")
+        w_rows = w_sb[:].rearrange("p (m k) -> p m k", m=4)
+        nc.scalar.dma_start(out=w_rows[:, 0:2, :], in_=W1.rearrange("(m p) k -> p m k", p=P))
+        nc.scalar.dma_start(out=w_rows[:, 2:4, :], in_=W2.rearrange("(m p) k -> p m k", p=P))
+        where = {}
+        for image, first, count in UNITS:
+            unit = xpool.tile([P, 4, count * CHUNK], BF16, name="x_%d_%d" % (image, first))
+            nc.sync.dma_start(
+                out=unit[:],
+                in_=x[image].rearrange("(p t) h w -> p t (h w)", t=4)[:, :, first * CHUNK : (first + count) * CHUNK],
+            )
+            for c in range(count):
+                where[4 * image + first + c] = (unit, c * CHUNK)
+
+        ident = const.tile([P, P], F32, name="ident")
+        make_identity(nc, ident[:])
+        w_words = w_sb[:].bitcast(F32).rearrange("p (m q u) -> p m u q", m=4, u=2)
+        w_grp = const.tile([P, 2048], BF16, name="w_grp", align_bytes=64)
+        w_grp_words = w_grp[:].bitcast(F32).rearrange("p (m o u) -> p m o u", m=4, u=2)
+        w_codes = const.tile([P, 512], U32, name="w_codes", align_bytes=64)
+        w_scales = const.tile([P, 512], U8, name="w_scales", align_bytes=64)
+        for h in range(2):
+            wt = psum.tile([P, 512], F32, name="wt", tag="c2", bufs=3)
+            wt_v = wt[:].rearrange("p (m u o) -> p m u o", m=2, u=2)
+            for mm in range(2):
+                for u in range(2):
+                    nc.tensor.transpose(wt_v[:, mm, u, :], w_words[:, 2 * h + mm, u, :], ident[:])
+            if h == 0:
+                nc.vector.tensor_copy(out=w_grp_words[:, 0:2], in_=wt_v.rearrange("p m u o -> p m o u"))
+            else:
+                nc.scalar.copy(out=w_grp_words[:, 2:4], in_=wt_v.rearrange("p m u o -> p m o u"))
+
+        grp = {}
+        codes = {}
+        scales = {}
+        c1 = {}
+        c2 = {}
+        sums = {}
+        mx = {}
+        o1 = {}
+        o2 = {}
+
+        def regroup(g):
+            unit, col = where[g]
+            grp[g] = gpool.tile([P, 4 * CHUNK], BF16, name="grp", align_bytes=64)
+            src = unit[:, :, col : col + CHUNK].rearrange("p t (i a j b) -> p a i j t b", i=8, a=2, j=16, b=2)
+            dst = grp[g][:].rearrange("p (a b i j t) -> p a i j t b", a=2, b=2, i=8, j=16, t=4)
+            nc.vector.tensor_copy(out=dst[:, 0], in_=src[:, 0])
+            nc.scalar.copy(out=dst[:, 1], in_=src[:, 1])
+
+        def quantise(g):
+            codes[g] = qpool.tile([P, CHUNK], U32, name="codes", align_bytes=64)
+            scales[g] = qpool.tile([P, CHUNK], U8, name="scales", align_bytes=64)
+            nc.vector.quantize_mx(out=codes[g][:].bitcast(FP8X4), scales=scales[g][:], in_=grp[g][:])
+
+        def mx_pass(out, m4, g, cols, start, stop):
+            nc.tensor.matmul_mx(
+                out=out,
+                lhsT=w_codes[:, m4 * P : (m4 + 1) * P].bitcast(FP8X4),
+                lhsT_scale=w_scales[:, m4 * P : (m4 + 1) * P],
+                rhs=codes[g][:, cols].bitcast(FP8X4),
+                rhs_scale=scales[g][:, cols],
+                start=start,
+                stop=stop,
+            )
+
+        def multiply(g):
+            whole = slice(0, CHUNK)
+            if g % 2 == 0:
+                sums[g // 2] = psum.tile([P, 512], F32, name="sums", tag="sums", bufs=2)
+            for m in range(2):
+                c1[(g, m)] = psum.tile([P, 512], F32, name="c1", tag="c1", bufs=3)
+                c2[(g, m)] = psum.tile([P, 512], F32, name="c2", tag="c2", bufs=3)
+            mx_pass(c1[(g, 0)][:], 0, g, whole, True, True)
+            mx_pass(c2[(g, 0)][:], 2, g, whole, True, True)
+            mx_pass(c2[(g, 1)][:], 3, g, whole, True, True)
+            mx_pass(c1[(g, 1)][:], 1, g, whole, True, True)
+            for m in range(2):
+                slot = 2 * m + g % 2
+                for q in range(4):
+                    mx_pass(sums[g // 2][:, slot * P : (slot + 1) * P], m, g, slice(q * P, (q + 1) * P), q == 0, q == 3)
+
+        def pool_part(g):
+            pair = g // 2
+            if g % 2 == 0:
+                mx[pair] = opool.tile([P, 512], F32, name="mx")
+            for m in range(2):
+                slot = 2 * m + g % 2
+                nc.vector.tensor_reduce(
+                    out=mx[pair][:, slot * P : (slot + 1) * P],
+                    in_=c1[(g, m)][:].rearrange("p (q n) -> p n q", q=4),
+                    axis=AXIS.X,
+                    op=ALU.max,
+                )
+            if g % 2 == 1:
+                image = g // 4
+                half = pair % 2
+                if half == 0:
+                    o1[image] = opool.tile([P, 2, 512], F32, name="o1")
+                nc.vector.scalar_tensor_tensor(
+                    out=o1[image][:, :, half * 256 : (half + 1) * 256],
+                    in0=sums[pair][:].rearrange("p (m n) -> p m n", m=2),
+                    scalar=0.25,
+                    in1=mx[pair][:].rearrange("p (m n) -> p m n", m=2),
+                    op0=ALU.mult,
+                    op1=ALU.add,
+                )
+
+        def copy_part(g):
+            pair = g // 2
+            for m in range(2):
+                if g % 2 == 0:
+                    o2[(pair, m)] = opool.tile([P, 2 * CHUNK], F32, name="o2", bufs=6)
+                dst = o2[(pair, m)][:, (g % 2) * CHUNK : (g % 2 + 1) * CHUNK].rearrange(
+                    "p (i a j b) -> p a i j b", i=8, a=2, j=16, b=2
+                )
+                src = c2[(g, m)][:].rearrange("p (a b i j) -> p a i j b", a=2, b=2, i=8, j=16)
+                for a in range(2):
+                    nc.scalar.copy(out=dst[:, a], in_=src[:, a])
+
+        def store(g):
+            if g % 2 == 0:
+                return
+            pair = g // 2
+            image = g // 4
+            half = pair % 2
+            for m in range(2):
+                nc.sync.dma_start(
+                    out=out_1[image].rearrange("(m p) h w -> p m (h w)", p=P)[:, m, half * 1024 : (half + 1) * 1024],
+                    in_=o2[(pair, m)][:],
+                )
+            if half == 1:
+                nc.sync.dma_start(out=out_0[image].rearrange("(m p) i j -> p m (i j)", p=P), in_=o1[image][:])
+
+        regroup(0)
+        nc.vector.quantize_mx(out=w_codes[:].bitcast(FP8X4), scales=w_scales[:], in_=w_grp[:])
+        regroup(1)
+        quantise(0)
+        multiply(0)
+        for g in range(N_CHUNKS):
+            if g + 2 < N_CHUNKS:
+                regroup(g + 2)
+            if g + 1 < N_CHUNKS:
+                quantise(g + 1)
+                multiply(g + 1)
+            pool_part(g)
+            copy_part(g)
+            store(g)

@@ -76,7 +76,13 @@ def tile_selfspatialattentionmodule_pa_t_kernel(tc, x, W1, W2, out_0, out_1):
             grp[g] = gpool.tile([P, 4 * CHUNK], BF16, name="grp", align_bytes=64)
             src = unit[:, :, col : col + CHUNK].rearrange("p t (i a j b) -> p a i j t b", i=8, a=2, j=16, b=2)
             dst = grp[g][:].rearrange("p (a b i j t) -> p a i j t b", a=2, b=2, i=8, j=16, t=4)
-            nc.vector.tensor_copy(out=dst[:, 0], in_=src[:, 0])
+            if g % 2 == 0:
+                nc.vector.tensor_copy(out=dst[:, 0], in_=src[:, 0])
+            else:
+                for b in range(2):
+                    nc.gpsimd.tensor_scalar(
+                        out=dst[:, 0, :, :, :, b], in0=src[:, 0, :, :, :, b], scalar1=1.0, scalar2=0.0, op0=ALU.mult, op1=ALU.add
+                    )
             nc.scalar.copy(out=dst[:, 1], in_=src[:, 1])
 
         def quantise(g):

@@ -16,6 +16,7 @@ AXIS = mybir.AxisListType
 P = 128
 CHUNK = 512
 N_CHUNKS = 16
+N_PAIRS = N_CHUNKS // 2
 UNITS = [(0, 0, 1), (0, 1, 1), (0, 2, 2), (1, 0, 4), (2, 0, 4), (3, 0, 4)]
 
 
@@ -50,17 +51,10 @@ def tile_selfspatialattentionmodule_pa_t_kernel(tc, x, W1, W2, out_0, out_1):
         w_grp_words = w_grp[:].bitcast(F32).rearrange("p (m o u) -> p m o u", m=4, u=2)
         w_codes = const.tile([P, 512], U32, name="w_codes", align_bytes=64)
         w_scales = const.tile([P, 512], U8, name="w_scales", align_bytes=64)
-        for h in range(2):
-            wt = psum.tile([P, 512], F32, name="wt", tag="c2", bufs=3)
-            wt_v = wt[:].rearrange("p (m u o) -> p m u o", m=2, u=2)
-            for mm in range(2):
-                for u in range(2):
-                    nc.tensor.transpose(wt_v[:, mm, u, :], w_words[:, 2 * h + mm, u, :], ident[:])
-            if h == 0:
-                nc.vector.tensor_copy(out=w_grp_words[:, 0:2], in_=wt_v.rearrange("p m u o -> p m o u"))
-            else:
-                nc.scalar.copy(out=w_grp_words[:, 2:4], in_=wt_v.rearrange("p m u o -> p m o u"))
 
+        ctx.enter_context(tc.manual_schedule())
+
+        wt = {}
         grp = {}
         codes = {}
         scales = {}
@@ -71,18 +65,44 @@ def tile_selfspatialattentionmodule_pa_t_kernel(tc, x, W1, W2, out_0, out_1):
         o1 = {}
         o2 = {}
 
-        def regroup(g):
+        def w_transpose(h):
+            wt[h] = psum.tile([P, 512], F32, name="wt", tag="c2", bufs=3)
+            wt_v = wt[h][:].rearrange("p (m u o) -> p m u o", m=2, u=2)
+            for mm in range(2):
+                for u in range(2):
+                    nc.tensor.transpose(wt_v[:, mm, u, :], w_words[:, 2 * h + mm, u, :], ident[:])
+
+        def w_copy(h):
+            nc.scalar.copy(
+                out=w_grp_words[:, 2 * h : 2 * h + 2], in_=wt[h][:].rearrange("p (m u o) -> p m o u", m=2, u=2)
+            )
+
+        def w_quantise(h):
+            nc.vector.quantize_mx(
+                out=w_codes[:, 256 * h : 256 * (h + 1)].bitcast(FP8X4),
+                scales=w_scales[:, 256 * h : 256 * (h + 1)],
+                in_=w_grp[:, 1024 * h : 1024 * (h + 1)],
+            )
+
+        def views(g):
             unit, col = where[g]
-            grp[g] = gpool.tile([P, 4 * CHUNK], BF16, name="grp", align_bytes=64)
             src = unit[:, :, col : col + CHUNK].rearrange("p t (i a j b) -> p a i j t b", i=8, a=2, j=16, b=2)
             dst = grp[g][:].rearrange("p (a b i j t) -> p a i j t b", a=2, b=2, i=8, j=16, t=4)
-            if g % 2 == 0:
+            return src, dst
+
+        def regroup_even_rows(g):
+            grp[g] = gpool.tile([P, 4 * CHUNK], BF16, name="grp", align_bytes=64)
+            src, dst = views(g)
+            if g % 2 == 0 or g == 1:
                 nc.vector.tensor_copy(out=dst[:, 0], in_=src[:, 0])
             else:
                 for b in range(2):
                     nc.gpsimd.tensor_scalar(
                         out=dst[:, 0, :, :, :, b], in0=src[:, 0, :, :, :, b], scalar1=1.0, scalar2=0.0, op0=ALU.mult, op1=ALU.add
                     )
+
+        def regroup_odd_rows(g):
+            src, dst = views(g)
             nc.scalar.copy(out=dst[:, 1], in_=src[:, 1])
 
         def quantise(g):
@@ -107,41 +127,47 @@ def tile_selfspatialattentionmodule_pa_t_kernel(tc, x, W1, W2, out_0, out_1):
                 sums[g // 2] = psum.tile([P, 512], F32, name="sums", tag="sums", bufs=2)
             for m in range(2):
                 c1[(g, m)] = psum.tile([P, 512], F32, name="c1", tag="c1", bufs=3)
+                mx_pass(c1[(g, m)][:], m, g, whole, True, True)
+            for m in range(2):
                 c2[(g, m)] = psum.tile([P, 512], F32, name="c2", tag="c2", bufs=3)
-            mx_pass(c1[(g, 0)][:], 0, g, whole, True, True)
-            mx_pass(c2[(g, 0)][:], 2, g, whole, True, True)
-            mx_pass(c2[(g, 1)][:], 3, g, whole, True, True)
-            mx_pass(c1[(g, 1)][:], 1, g, whole, True, True)
+                mx_pass(c2[(g, m)][:], 2 + m, g, whole, True, True)
             for m in range(2):
                 slot = 2 * m + g % 2
                 for q in range(4):
                     mx_pass(sums[g // 2][:, slot * P : (slot + 1) * P], m, g, slice(q * P, (q + 1) * P), q == 0, q == 3)
 
-        def pool_part(g):
+        def pool_max(g, m):
             pair = g // 2
-            if g % 2 == 0:
+            if g % 2 == 0 and m == 0:
                 mx[pair] = opool.tile([P, 512], F32, name="mx")
-            for m in range(2):
-                slot = 2 * m + g % 2
-                nc.vector.tensor_reduce(
-                    out=mx[pair][:, slot * P : (slot + 1) * P],
-                    in_=c1[(g, m)][:].rearrange("p (q n) -> p n q", q=4),
-                    axis=AXIS.X,
-                    op=ALU.max,
+            slot = 2 * m + g % 2
+            nc.vector.tensor_reduce(
+                out=mx[pair][:, slot * P : (slot + 1) * P],
+                in_=c1[(g, m)][:].rearrange("p (q n) -> p n q", q=4),
+                axis=AXIS.X,
+                op=ALU.max,
+            )
+
+        def pool_finish(pair):
+            image = pair // 2
+            half = pair % 2
+            if half == 0:
+                o1[image] = opool.tile([P, 2, 512], F32, name="o1")
+            nc.vector.scalar_tensor_tensor(
+                out=o1[image][:, :, half * 256 : (half + 1) * 256],
+                in0=sums[pair][:].rearrange("p (m n) -> p m n", m=2),
+                scalar=0.25,
+                in1=mx[pair][:].rearrange("p (m n) -> p m n", m=2),
+                op0=ALU.mult,
+                op1=ALU.add,
+            )
+            c1p_rows = out_0[image].rearrange("(m p) i j -> p m (i j)", p=P)
+            if image == 3:
+                nc.sync.dma_start(
+                    out=c1p_rows[:, :, half * 256 : (half + 1) * 256], in_=o1[image][:, :, half * 256 : (half + 1) * 256]
                 )
-            if g % 2 == 1:
-                image = g // 4
-                half = pair % 2
-                if half == 0:
-                    o1[image] = opool.tile([P, 2, 512], F32, name="o1")
-                nc.vector.scalar_tensor_tensor(
-                    out=o1[image][:, :, half * 256 : (half + 1) * 256],
-                    in0=sums[pair][:].rearrange("p (m n) -> p m n", m=2),
-                    scalar=0.25,
-                    in1=mx[pair][:].rearrange("p (m n) -> p m n", m=2),
-                    op0=ALU.mult,
-                    op1=ALU.add,
-                )
+            elif half == 1:
+                nc.sync.dma_start(out=c1p_rows, in_=o1[image][:])
 
         def copy_part(g):
             pair = g // 2
@@ -152,34 +178,48 @@ def tile_selfspatialattentionmodule_pa_t_kernel(tc, x, W1, W2, out_0, out_1):
                     "p (i a j b) -> p a i j b", i=8, a=2, j=16, b=2
                 )
                 src = c2[(g, m)][:].rearrange("p (a b i j) -> p a i j b", a=2, b=2, i=8, j=16)
-                for a in range(2):
-                    nc.scalar.copy(out=dst[:, a], in_=src[:, a])
+                nc.scalar.copy(out=dst, in_=src)
 
         def store(g):
-            if g % 2 == 0:
-                return
             pair = g // 2
             image = g // 4
             half = pair % 2
-            for m in range(2):
-                nc.sync.dma_start(
-                    out=out_1[image].rearrange("(m p) h w -> p m (h w)", p=P)[:, m, half * 1024 : (half + 1) * 1024],
-                    in_=o2[(pair, m)][:],
-                )
-            if half == 1:
-                nc.sync.dma_start(out=out_0[image].rearrange("(m p) i j -> p m (i j)", p=P), in_=o1[image][:])
+            c2_rows = out_1[image].rearrange("(m p) h w -> p m (h w)", p=P)
+            if pair == N_PAIRS - 1:
+                first = (g % 4) * CHUNK
+                for m in range(2):
+                    nc.sync.dma_start(
+                        out=c2_rows[:, m, first : first + CHUNK], in_=o2[(pair, m)][:, (g % 2) * CHUNK : (g % 2 + 1) * CHUNK]
+                    )
+            elif g % 2 == 1:
+                for m in range(2):
+                    nc.sync.dma_start(out=c2_rows[:, m, half * 1024 : (half + 1) * 1024], in_=o2[(pair, m)][:])
 
-        regroup(0)
-        nc.vector.quantize_mx(out=w_codes[:].bitcast(FP8X4), scales=w_scales[:], in_=w_grp[:])
-        regroup(1)
+        w_transpose(0)
+        w_transpose(1)
+        regroup_even_rows(0)
+        regroup_odd_rows(0)
+        w_copy(0)
         quantise(0)
+        w_quantise(0)
+        regroup_even_rows(1)
+        regroup_odd_rows(1)
+        w_copy(1)
+        quantise(1)
+        w_quantise(1)
         multiply(0)
+        multiply(1)
         for g in range(N_CHUNKS):
-            if g + 2 < N_CHUNKS:
-                regroup(g + 2)
-            if g + 1 < N_CHUNKS:
+            if 1 <= g and g + 1 < N_CHUNKS:
                 quantise(g + 1)
                 multiply(g + 1)
-            pool_part(g)
+            if g % 2 == 0 and g >= 2:
+                pool_finish(g // 2 - 1)
+            pool_max(g, 0)
+            if g + 2 < N_CHUNKS:
+                regroup_even_rows(g + 2)
+                regroup_odd_rows(g + 2)
+            pool_max(g, 1)
             copy_part(g)
             store(g)
+        pool_finish(N_PAIRS - 1)

@@ -17,6 +17,7 @@ P = 128
 CHUNK = 512
 N_CHUNKS = 16
 N_PAIRS = N_CHUNKS // 2
+WARM_UP = 6
 UNITS = [(0, 0, 1), (0, 1, 1), (0, 2, 2), (1, 0, 4), (2, 0, 4), (3, 0, 4)]
 
 
@@ -51,6 +52,9 @@ def tile_selfspatialattentionmodule_pa_t_kernel(tc, x, W1, W2, out_0, out_1):
         w_grp_words = w_grp[:].bitcast(F32).rearrange("p (m o u) -> p m o u", m=4, u=2)
         w_codes = const.tile([P, 512], U32, name="w_codes", align_bytes=64)
         w_scales = const.tile([P, 512], U8, name="w_scales", align_bytes=64)
+
+        warm = const.tile([P, 512], BF16, name="warm")
+        nc.vector.memset(warm[:], 0.0)
 
         ctx.enter_context(tc.manual_schedule())
 
@@ -127,10 +131,14 @@ def tile_selfspatialattentionmodule_pa_t_kernel(tc, x, W1, W2, out_0, out_1):
                 sums[g // 2] = psum.tile([P, 512], F32, name="sums", tag="sums", bufs=2)
             for m in range(2):
                 c1[(g, m)] = psum.tile([P, 512], F32, name="c1", tag="c1", bufs=3)
-                mx_pass(c1[(g, m)][:], m, g, whole, True, True)
-            for m in range(2):
                 c2[(g, m)] = psum.tile([P, 512], F32, name="c2", tag="c2", bufs=3)
-                mx_pass(c2[(g, m)][:], 2 + m, g, whole, True, True)
+            mx_pass(c1[(g, 0)][:], 0, g, whole, True, True)
+            if g == 0:
+                mx_pass(c1[(g, 1)][:], 1, g, whole, True, True)
+            mx_pass(c2[(g, 0)][:], 2, g, whole, True, True)
+            mx_pass(c2[(g, 1)][:], 3, g, whole, True, True)
+            if g > 0:
+                mx_pass(c1[(g, 1)][:], 1, g, whole, True, True)
             for m in range(2):
                 slot = 2 * m + g % 2
                 for q in range(4):
@@ -152,7 +160,7 @@ def tile_selfspatialattentionmodule_pa_t_kernel(tc, x, W1, W2, out_0, out_1):
             image = pair // 2
             half = pair % 2
             if half == 0:
-                o1[image] = opool.tile([P, 2, 512], F32, name="o1")
+                o1[image] = opool.tile([P, 2, 512], F32, name="o1", bufs=4)
             nc.vector.scalar_tensor_tensor(
                 out=o1[image][:, :, half * 256 : (half + 1) * 256],
                 in0=sums[pair][:].rearrange("p (m n) -> p m n", m=2),
@@ -173,7 +181,7 @@ def tile_selfspatialattentionmodule_pa_t_kernel(tc, x, W1, W2, out_0, out_1):
             pair = g // 2
             for m in range(2):
                 if g % 2 == 0:
-                    o2[(pair, m)] = opool.tile([P, 2 * CHUNK], F32, name="o2", bufs=6)
+                    o2[(pair, m)] = opool.tile([P, 2 * CHUNK], F32, name="o2", bufs=12)
                 dst = o2[(pair, m)][:, (g % 2) * CHUNK : (g % 2 + 1) * CHUNK].rearrange(
                     "p (i a j b) -> p a i j b", i=8, a=2, j=16, b=2
                 )
@@ -195,6 +203,9 @@ def tile_selfspatialattentionmodule_pa_t_kernel(tc, x, W1, W2, out_0, out_1):
                 for m in range(2):
                     nc.sync.dma_start(out=c2_rows[:, m, half * 1024 : (half + 1) * 1024], in_=o2[(pair, m)][:])
 
+        for n in range(WARM_UP):
+            idle = psum.tile([P, 512], F32, name="idle", tag="c1", bufs=3)
+            nc.tensor.matmul(out=idle[:], lhsT=warm[:, 0:P], rhs=warm[:], start=True, stop=True)
         w_transpose(0)
         w_transpose(1)
         regroup_even_rows(0)
@@ -213,12 +224,12 @@ def tile_selfspatialattentionmodule_pa_t_kernel(tc, x, W1, W2, out_0, out_1):
             if 1 <= g and g + 1 < N_CHUNKS:
                 quantise(g + 1)
                 multiply(g + 1)
-            if g % 2 == 0 and g >= 2:
-                pool_finish(g // 2 - 1)
-            pool_max(g, 0)
             if g + 2 < N_CHUNKS:
                 regroup_even_rows(g + 2)
                 regroup_odd_rows(g + 2)
+            if g % 2 == 0 and g >= 2:
+                pool_finish(g // 2 - 1)
+            pool_max(g, 0)
             pool_max(g, 1)
             copy_part(g)
             store(g)

@@ -17,7 +17,7 @@ P = 128
 CHUNK = 512
 N_CHUNKS = 16
 N_PAIRS = N_CHUNKS // 2
-WARM_UP = 6
+WARM_UP = 5
 UNITS = [(0, 0, 1), (0, 1, 1), (0, 2, 2), (1, 0, 4), (2, 0, 4), (3, 0, 4)]
 
 
@@ -33,8 +33,6 @@ def tile_selfspatialattentionmodule_pa_t_kernel(tc, x, W1, W2, out_0, out_1):
 
         w_sb = const.tile([P, 4 * 512], BF16, name="w_sb")
         w_rows = w_sb[:].rearrange("p (m k) -> p m k", m=4)
-        nc.scalar.dma_start(out=w_rows[:, 0:2, :], in_=W1.rearrange("(m p) k -> p m k", p=P))
-        nc.scalar.dma_start(out=w_rows[:, 2:4, :], in_=W2.rearrange("(m p) k -> p m k", p=P))
         where = {}
         for image, first, count in UNITS:
             unit = xpool.tile([P, 4, count * CHUNK], BF16, name="x_%d_%d" % (image, first))
@@ -44,6 +42,9 @@ def tile_selfspatialattentionmodule_pa_t_kernel(tc, x, W1, W2, out_0, out_1):
             )
             for c in range(count):
                 where[4 * image + first + c] = (unit, c * CHUNK)
+            if image == 0 and first == 0:
+                nc.sync.dma_start(out=w_rows[:, 0:2, :], in_=W1.rearrange("(m p) k -> p m k", p=P))
+                nc.sync.dma_start(out=w_rows[:, 2:4, :], in_=W2.rearrange("(m p) k -> p m k", p=P))
 
         ident = const.tile([P, P], F32, name="ident")
         make_identity(nc, ident[:])
@@ -107,7 +108,10 @@ def tile_selfspatialattentionmodule_pa_t_kernel(tc, x, W1, W2, out_0, out_1):
 
         def regroup_odd_rows(g):
             src, dst = views(g)
-            nc.scalar.copy(out=dst[:, 1], in_=src[:, 1])
+            if g == 0:
+                nc.vector.tensor_copy(out=dst[:, 1], in_=src[:, 1])
+            else:
+                nc.scalar.copy(out=dst[:, 1], in_=src[:, 1])
 
         def quantise(g):
             codes[g] = qpool.tile([P, CHUNK], U32, name="codes", align_bytes=64)
@@ -211,17 +215,18 @@ def tile_selfspatialattentionmodule_pa_t_kernel(tc, x, W1, W2, out_0, out_1):
         regroup_even_rows(0)
         regroup_odd_rows(0)
         w_copy(0)
+        w_copy(1)
         quantise(0)
         w_quantise(0)
-        regroup_even_rows(1)
-        regroup_odd_rows(1)
-        w_copy(1)
-        quantise(1)
         w_quantise(1)
         multiply(0)
-        multiply(1)
+        regroup_even_rows(1)
+        regroup_odd_rows(1)
         for g in range(N_CHUNKS):
-            if 1 <= g and g + 1 < N_CHUNKS:
+            if g == 0:
+                pool_max(g, 0)
+                pool_max(g, 1)
+            if g + 1 < N_CHUNKS:
                 quantise(g + 1)
                 multiply(g + 1)
             if g + 2 < N_CHUNKS:
@@ -229,8 +234,9 @@ def tile_selfspatialattentionmodule_pa_t_kernel(tc, x, W1, W2, out_0, out_1):
                 regroup_odd_rows(g + 2)
             if g % 2 == 0 and g >= 2:
                 pool_finish(g // 2 - 1)
-            pool_max(g, 0)
-            pool_max(g, 1)
+            if g >= 1:
+                pool_max(g, 0)
+                pool_max(g, 1)
             copy_part(g)
             store(g)
         pool_finish(N_PAIRS - 1)

@@ -91,6 +91,12 @@ def tile_selfspatialattentionmodule_pa_t_kernel(tc, x, W1, W2, out_0, out_1):
 
         def views(g):
             unit, col = where[g]
+            src = unit[:, :, col : col + CHUNK].rearrange("p t (i a j e b) -> p a i j t e b", i=8, a=2, j=8, e=2, b=2)
+            dst = grp[g][:].rearrange("p (a b i j e t) -> p a i j t e b", a=2, b=2, i=8, j=8, e=2, t=4)
+            return src, dst
+
+        def single_views(g):
+            unit, col = where[g]
             src = unit[:, :, col : col + CHUNK].rearrange("p t (i a j b) -> p a i j t b", i=8, a=2, j=16, b=2)
             dst = grp[g][:].rearrange("p (a b i j t) -> p a i j t b", a=2, b=2, i=8, j=16, t=4)
             return src, dst
@@ -101,6 +107,7 @@ def tile_selfspatialattentionmodule_pa_t_kernel(tc, x, W1, W2, out_0, out_1):
             if g % 2 == 0 or g == 1:
                 nc.vector.tensor_copy(out=dst[:, 0], in_=src[:, 0])
             else:
+                src, dst = single_views(g)
                 for b in range(2):
                     nc.gpsimd.tensor_scalar(
                         out=dst[:, 0, :, :, :, b], in0=src[:, 0, :, :, :, b], scalar1=1.0, scalar2=0.0, op0=ALU.mult, op1=ALU.add

@@ -17,8 +17,9 @@ P = 128
 CHUNK = 512
 N_CHUNKS = 16
 N_PAIRS = N_CHUNKS // 2
+FINE_PAIR = 5
 WARM_UP = 5
-UNITS = [(0, 0, 1), (0, 1, 1), (0, 2, 2), (1, 0, 4), (2, 0, 4), (3, 0, 4)]
+UNITS = [(0, 0, 1), (0, 1, 1), (0, 2, 1), (0, 3, 1), (1, 0, 2), (1, 2, 2), (2, 0, 4), (3, 0, 4)]
 
 
 def tile_selfspatialattentionmodule_pa_t_kernel(tc, x, W1, W2, out_0, out_1):
@@ -53,6 +54,9 @@ def tile_selfspatialattentionmodule_pa_t_kernel(tc, x, W1, W2, out_0, out_1):
         w_grp_words = w_grp[:].bitcast(F32).rearrange("p (m o u) -> p m o u", m=4, u=2)
         w_codes = const.tile([P, 512], U32, name="w_codes", align_bytes=64)
         w_scales = const.tile([P, 512], U8, name="w_scales", align_bytes=64)
+        v_grp = const.tile([P, 1024], BF16, name="v_grp", align_bytes=64)
+        v_codes = const.tile([P, 256], U32, name="v_codes", align_bytes=64)
+        v_scales = const.tile([P, 256], U8, name="v_scales", align_bytes=64)
 
         warm = const.tile([P, 512], BF16, name="warm")
         nc.vector.memset(warm[:], 0.0)
@@ -88,6 +92,13 @@ def tile_selfspatialattentionmodule_pa_t_kernel(tc, x, W1, W2, out_0, out_1):
                 scales=w_scales[:, 256 * h : 256 * (h + 1)],
                 in_=w_grp[:, 1024 * h : 1024 * (h + 1)],
             )
+
+        def variants():
+            nc.vector.tensor_scalar_mul(v_grp[:, 0:512], w_grp[:, 0:512], -1.0)
+            nc.vector.tensor_scalar_mul(v_grp[:, 512:1024], w_grp[:, 0:512], 0.25)
+
+        def variants_quantise():
+            nc.vector.quantize_mx(out=v_codes[:].bitcast(FP8X4), scales=v_scales[:], in_=v_grp[:])
 
         def views(g):
             unit, col = where[g]
@@ -126,10 +137,11 @@ def tile_selfspatialattentionmodule_pa_t_kernel(tc, x, W1, W2, out_0, out_1):
             nc.vector.quantize_mx(out=codes[g][:].bitcast(FP8X4), scales=scales[g][:], in_=grp[g][:])
 
         def mx_pass(out, m4, g, cols, start, stop):
+            w, ws, at = (w_codes, w_scales, m4 * P) if m4 < 4 else (v_codes, v_scales, (m4 - 4) * P)
             nc.tensor.matmul_mx(
                 out=out,
-                lhsT=w_codes[:, m4 * P : (m4 + 1) * P].bitcast(FP8X4),
-                lhsT_scale=w_scales[:, m4 * P : (m4 + 1) * P],
+                lhsT=w[:, at : at + P].bitcast(FP8X4),
+                lhsT_scale=ws[:, at : at + P],
                 rhs=codes[g][:, cols].bitcast(FP8X4),
                 rhs_scale=scales[g][:, cols],
                 start=start,
@@ -143,48 +155,65 @@ def tile_selfspatialattentionmodule_pa_t_kernel(tc, x, W1, W2, out_0, out_1):
             for m in range(2):
                 c1[(g, m)] = psum.tile([P, 512], F32, name="c1", tag="c1", bufs=3)
                 c2[(g, m)] = psum.tile([P, 512], F32, name="c2", tag="c2", bufs=3)
-            mx_pass(c1[(g, 0)][:], 0, g, whole, True, True)
+            last = g == N_CHUNKS - 1
+            plane = [slice(q * P, (q + 1) * P) for q in range(4)]
+            if last:
+                mx_pass(c2[(g, 0)][:], 2, g, whole, True, True)
+                mx_pass(c2[(g, 1)][:], 3, g, whole, True, True)
+            if g < 2:
+                mx_pass(c1[(g, 0)][:], 0, g, whole, True, True)
+            else:
+                for q in range(3):
+                    mx_pass(c1[(g, 0)][:, plane[q]], 0, g, plane[q], True, False)
+                    mx_pass(c1[(g, 0)][:, plane[q]], 4, g, plane[3], False, True)
             if g == 0:
                 mx_pass(c1[(g, 1)][:], 1, g, whole, True, True)
-            mx_pass(c2[(g, 0)][:], 2, g, whole, True, True)
-            mx_pass(c2[(g, 1)][:], 3, g, whole, True, True)
+            if not last:
+                mx_pass(c2[(g, 0)][:], 2, g, whole, True, True)
+                mx_pass(c2[(g, 1)][:], 3, g, whole, True, True)
             if g > 0:
                 mx_pass(c1[(g, 1)][:], 1, g, whole, True, True)
             for m in range(2):
                 slot = 2 * m + g % 2
-                for q in range(4):
-                    mx_pass(sums[g // 2][:, slot * P : (slot + 1) * P], m, g, slice(q * P, (q + 1) * P), q == 0, q == 3)
+                terms = [(m, q) for q in range(4)] if m == 1 or g < 2 else [(0, 3)] + [(5, q) for q in range(4)]
+                for n, (slab, q) in enumerate(terms):
+                    mx_pass(
+                        sums[g // 2][:, slot * P : (slot + 1) * P], slab, g, plane[q], n == 0, n == len(terms) - 1
+                    )
 
         def pool_max(g, m):
             pair = g // 2
             if g % 2 == 0 and m == 0:
                 mx[pair] = opool.tile([P, 512], F32, name="mx")
             slot = 2 * m + g % 2
+            planes = 4 if m == 1 or g < 2 else 3
             nc.vector.tensor_reduce(
                 out=mx[pair][:, slot * P : (slot + 1) * P],
-                in_=c1[(g, m)][:].rearrange("p (q n) -> p n q", q=4),
+                in_=c1[(g, m)][:, 0 : planes * P].rearrange("p (q n) -> p n q", q=planes),
                 axis=AXIS.X,
                 op=ALU.max,
             )
 
-        def pool_finish(pair):
+        def pool_finish(pair, slabs):
             image = pair // 2
             half = pair % 2
+            here = slice(half * 256, (half + 1) * 256)
             if half == 0:
                 o1[image] = opool.tile([P, 2, 512], F32, name="o1", bufs=4)
-            nc.vector.scalar_tensor_tensor(
-                out=o1[image][:, :, half * 256 : (half + 1) * 256],
-                in0=sums[pair][:].rearrange("p (m n) -> p m n", m=2),
-                scalar=0.25,
-                in1=mx[pair][:].rearrange("p (m n) -> p m n", m=2),
-                op0=ALU.mult,
-                op1=ALU.add,
-            )
+            for m in slabs:
+                cols = slice(m * 256, (m + 1) * 256)
+                if m == 0 and pair > 0:
+                    nc.vector.scalar_tensor_tensor(
+                        out=o1[image][:, m, here], in0=mx[pair][:, cols], scalar=0.0, in1=sums[pair][:, cols], op0=ALU.max, op1=ALU.add
+                    )
+                else:
+                    nc.vector.scalar_tensor_tensor(
+                        out=o1[image][:, m, here], in0=sums[pair][:, cols], scalar=0.25, in1=mx[pair][:, cols], op0=ALU.mult, op1=ALU.add
+                    )
+            part = slice(slabs[0], slabs[-1] + 1)
             c1p_rows = out_0[image].rearrange("(m p) i j -> p m (i j)", p=P)
             if image == 3:
-                nc.sync.dma_start(
-                    out=c1p_rows[:, :, half * 256 : (half + 1) * 256], in_=o1[image][:, :, half * 256 : (half + 1) * 256]
-                )
+                nc.sync.dma_start(out=c1p_rows[:, part, here], in_=o1[image][:, part, here])
             elif half == 1:
                 nc.sync.dma_start(out=c1p_rows, in_=o1[image][:])
 
@@ -204,7 +233,7 @@ def tile_selfspatialattentionmodule_pa_t_kernel(tc, x, W1, W2, out_0, out_1):
             image = g // 4
             half = pair % 2
             c2_rows = out_1[image].rearrange("(m p) h w -> p m (h w)", p=P)
-            if pair == N_PAIRS - 1:
+            if pair >= FINE_PAIR:
                 first = (g % 4) * CHUNK
                 for m in range(2):
                     nc.sync.dma_start(
@@ -225,14 +254,16 @@ def tile_selfspatialattentionmodule_pa_t_kernel(tc, x, W1, W2, out_0, out_1):
         w_copy(1)
         quantise(0)
         w_quantise(0)
-        w_quantise(1)
-        multiply(0)
         regroup_even_rows(1)
         regroup_odd_rows(1)
+        variants()
+        w_quantise(1)
+        multiply(0)
         for g in range(N_CHUNKS):
             if g == 0:
                 pool_max(g, 0)
                 pool_max(g, 1)
+                variants_quantise()
             if g + 1 < N_CHUNKS:
                 quantise(g + 1)
                 multiply(g + 1)
@@ -240,10 +271,11 @@ def tile_selfspatialattentionmodule_pa_t_kernel(tc, x, W1, W2, out_0, out_1):
                 regroup_even_rows(g + 2)
                 regroup_odd_rows(g + 2)
             if g % 2 == 0 and g >= 2:
-                pool_finish(g // 2 - 1)
+                pool_finish(g // 2 - 1, (0, 1))
+            copy_part(g)
+            store(g)
             if g >= 1:
                 pool_max(g, 0)
                 pool_max(g, 1)
-            copy_part(g)
-            store(g)
-        pool_finish(N_PAIRS - 1)
+        for m in range(2):
+            pool_finish(N_PAIRS - 1, (m,))

@@ -19,6 +19,7 @@ N_CHUNKS = 16
 N_PAIRS = N_CHUNKS // 2
 FINE_PAIR = 5
 WARM_UP = 5
+KEEP_WARM = 3
 UNITS = [(0, 0, 1), (0, 1, 1), (0, 2, 1), (0, 3, 1), (1, 0, 2), (1, 2, 2), (2, 0, 4), (3, 0, 4)]
 
 
@@ -243,11 +244,15 @@ def tile_selfspatialattentionmodule_pa_t_kernel(tc, x, W1, W2, out_0, out_1):
                 for m in range(2):
                     nc.sync.dma_start(out=c2_rows[:, m, half * 1024 : (half + 1) * 1024], in_=o2[(pair, m)][:])
 
-        for n in range(WARM_UP):
-            idle = psum.tile([P, 512], F32, name="idle", tag="c1", bufs=3)
-            nc.tensor.matmul(out=idle[:], lhsT=warm[:, 0:P], rhs=warm[:], start=True, stop=True)
+        def dummies(count):
+            for n in range(count):
+                idle = psum.tile([P, 512], F32, name="idle", tag="c1", bufs=3)
+                nc.tensor.matmul(out=idle[:], lhsT=warm[:, 0:P], rhs=warm[:], start=True, stop=True)
+
+        dummies(WARM_UP)
         w_transpose(0)
         w_transpose(1)
+        dummies(KEEP_WARM)
         regroup_even_rows(0)
         regroup_odd_rows(0)
         w_copy(0)

from contextlib import ExitStack

import concourse.mybir as mybir
from concourse.masks import make_identity

FLOPS = 2 * 512 * 512 * 8192

F32 = mybir.dt.float32
BF16 = mybir.dt.bfloat16
U32 = mybir.dt.uint32
U8 = mybir.dt.uint8
FP8X4 = mybir.dt.float8_e4m3fn_x4
ALU = mybir.AluOpType
AXIS = mybir.AxisListType

P = 128
CHUNK = 512
N_CHUNKS = 16
N_PAIRS = N_CHUNKS // 2
FINE_PAIR = 5
WARM_UP = 5
KEEP_WARM = 3
UNITS = [(0, 0, 1), (0, 1, 1), (0, 2, 1), (0, 3, 1), (1, 0, 2), (1, 2, 2), (2, 0, 4), (3, 0, 4)]


def tile_selfspatialattentionmodule_pa_t_kernel(tc, x, W1, W2, out_0, out_1):
    nc = tc.nc
    with ExitStack() as ctx:
        const = ctx.enter_context(tc.tile_pool(name="const", bufs=1))
        xpool = ctx.enter_context(tc.tile_pool(name="xpool", bufs=1))
        gpool = ctx.enter_context(tc.tile_pool(name="gpool", bufs=4))
        qpool = ctx.enter_context(tc.tile_pool(name="qpool", bufs=4))
        opool = ctx.enter_context(tc.tile_pool(name="opool", bufs=2))
        psum = ctx.enter_context(tc.psum_pool(name="psum", bufs=2))

        w_sb = const.tile([P, 4 * 512], BF16, name="w_sb")
        w_rows = w_sb[:].rearrange("p (m k) -> p m k", m=4)
        where = {}
        for image, first, count in UNITS:
            unit = xpool.tile([P, 4, count * CHUNK], BF16, name="x_%d_%d" % (image, first))
            nc.sync.dma_start(
                out=unit[:],
                in_=x[image].rearrange("(p t) h w -> p t (h w)", t=4)[:, :, first * CHUNK : (first + count) * CHUNK],
            )
            for c in range(count):
                where[4 * image + first + c] = (unit, c * CHUNK)
            if image == 0 and first == 0:
                nc.sync.dma_start(out=w_rows[:, 0:2, :], in_=W1.rearrange("(m p) k -> p m k", p=P))
                nc.sync.dma_start(out=w_rows[:, 2:4, :], in_=W2.rearrange("(m p) k -> p m k", p=P))

        ident = const.tile([P, P], F32, name="ident")
        make_identity(nc, ident[:])
        w_words = w_sb[:].bitcast(F32).rearrange("p (m q u) -> p m u q", m=4, u=2)
        w_grp = const.tile([P, 2048], BF16, name="w_grp", align_bytes=64)
        w_grp_words = w_grp[:].bitcast(F32).rearrange("p (m o u) -> p m o u", m=4, u=2)
        w_codes = const.tile([P, 512], U32, name="w_codes", align_bytes=64)
        w_scales = const.tile([P, 512], U8, name="w_scales", align_bytes=64)
        v_grp = const.tile([P, 1024], BF16, name="v_grp", align_bytes=64)
        v_codes = const.tile([P, 256], U32, name="v_codes", align_bytes=64)
        v_scales = const.tile([P, 256], U8, name="v_scales", align_bytes=64)

        warm = const.tile([P, 512], BF16, name="warm")
        nc.vector.memset(warm[:], 0.0)

        ctx.enter_context(tc.manual_schedule())

        wt = {}
        grp = {}
        codes = {}
        scales = {}
        c1 = {}
        c2 = {}
        sums = {}
        mx = {}
        o1 = {}
        o2 = {}

        def w_transpose(h):
            wt[h] = psum.tile([P, 512], F32, name="wt", tag="c2", bufs=3)
            wt_v = wt[h][:].rearrange("p (m u o) -> p m u o", m=2, u=2)
            for mm in range(2):
                for u in range(2):
                    nc.tensor.transpose(wt_v[:, mm, u, :], w_words[:, 2 * h + mm, u, :], ident[:])

        def w_copy(h):
            nc.scalar.copy(
                out=w_grp_words[:, 2 * h : 2 * h + 2], in_=wt[h][:].rearrange("p (m u o) -> p m o u", m=2, u=2)
            )

        def w_quantise(h):
            nc.vector.quantize_mx(
                out=w_codes[:, 256 * h : 256 * (h + 1)].bitcast(FP8X4),
                scales=w_scales[:, 256 * h : 256 * (h + 1)],
                in_=w_grp[:, 1024 * h : 1024 * (h + 1)],
            )

        def variants():
            nc.vector.tensor_scalar_mul(v_grp[:, 0:512], w_grp[:, 0:512], -1.0)
            nc.vector.tensor_scalar_mul(v_grp[:, 512:1024], w_grp[:, 0:512], 0.25)

        def variants_quantise():
            nc.vector.quantize_mx(out=v_codes[:].bitcast(FP8X4), scales=v_scales[:], in_=v_grp[:])

        def views(g):
            unit, col = where[g]
            src = unit[:, :, col : col + CHUNK].rearrange("p t (i a j e b) -> p a i j t e b", i=8, a=2, j=8, e=2, b=2)
            dst = grp[g][:].rearrange("p (a b i j e t) -> p a i j t e b", a=2, b=2, i=8, j=8, e=2, t=4)
            return src, dst

        def single_views(g):
            unit, col = where[g]
            src = unit[:, :, col : col + CHUNK].rearrange("p t (i a j b) -> p a i j t b", i=8, a=2, j=16, b=2)
            dst = grp[g][:].rearrange("p (a b i j t) -> p a i j t b", a=2, b=2, i=8, j=16, t=4)
            return src, dst

        def regroup_even_rows(g):
            grp[g] = gpool.tile([P, 4 * CHUNK], BF16, name="grp", align_bytes=64)
            src, dst = views(g)
            if g % 2 == 0 or g == 1:
                nc.vector.tensor_copy(out=dst[:, 0], in_=src[:, 0])
            else:
                src, dst = single_views(g)
                for b in range(2):
                    nc.gpsimd.tensor_scalar(
                        out=dst[:, 0, :, :, :, b], in0=src[:, 0, :, :, :, b], scalar1=1.0, scalar2=0.0, op0=ALU.mult, op1=ALU.add
                    )

        def regroup_odd_rows(g):
            src, dst = views(g)
            if g == 0:
                nc.vector.tensor_copy(out=dst[:, 1], in_=src[:, 1])
            else:
                nc.scalar.copy(out=dst[:, 1], in_=src[:, 1])

        def quantise(g):
            codes[g] = qpool.tile([P, CHUNK], U32, name="codes", align_bytes=64)
            scales[g] = qpool.tile([P, CHUNK], U8, name="scales", align_bytes=64)
            nc.vector.quantize_mx(out=codes[g][:].bitcast(FP8X4), scales=scales[g][:], in_=grp[g][:])

        def mx_pass(out, m4, g, cols, start, stop):
            w, ws, at = (w_codes, w_scales, m4 * P) if m4 < 4 else (v_codes, v_scales, (m4 - 4) * P)
            nc.tensor.matmul_mx(
                out=out,
                lhsT=w[:, at : at + P].bitcast(FP8X4),
                lhsT_scale=ws[:, at : at + P],
                rhs=codes[g][:, cols].bitcast(FP8X4),
                rhs_scale=scales[g][:, cols],
                start=start,
                stop=stop,
            )

        def multiply(g):
            whole = slice(0, CHUNK)
            if g % 2 == 0:
                sums[g // 2] = psum.tile([P, 512], F32, name="sums", tag="sums", bufs=2)
            for m in range(2):
                c1[(g, m)] = psum.tile([P, 512], F32, name="c1", tag="c1", bufs=3)
                c2[(g, m)] = psum.tile([P, 512], F32, name="c2", tag="c2", bufs=3)
            last = g == N_CHUNKS - 1
            plane = [slice(q * P, (q + 1) * P) for q in range(4)]
            if last:
                mx_pass(c2[(g, 0)][:], 2, g, whole, True, True)
                mx_pass(c2[(g, 1)][:], 3, g, whole, True, True)
            if g < 2:
                mx_pass(c1[(g, 0)][:], 0, g, whole, True, True)
            else:
                for q in range(3):
                    mx_pass(c1[(g, 0)][:, plane[q]], 0, g, plane[q], True, False)
                    mx_pass(c1[(g, 0)][:, plane[q]], 4, g, plane[3], False, True)
            if g == 0:
                mx_pass(c1[(g, 1)][:], 1, g, whole, True, True)
            if not last:
                mx_pass(c2[(g, 0)][:], 2, g, whole, True, True)
                mx_pass(c2[(g, 1)][:], 3, g, whole, True, True)
            if g > 0:
                mx_pass(c1[(g, 1)][:], 1, g, whole, True, True)
            for m in range(2):
                slot = 2 * m + g % 2
                terms = [(m, q) for q in range(4)] if m == 1 or g < 2 else [(0, 3)] + [(5, q) for q in range(4)]
                for n, (slab, q) in enumerate(terms):
                    mx_pass(
                        sums[g // 2][:, slot * P : (slot + 1) * P], slab, g, plane[q], n == 0, n == len(terms) - 1
                    )

        def pool_max(g, m):
            pair = g // 2
            if g % 2 == 0 and m == 0:
                mx[pair] = opool.tile([P, 512], F32, name="mx")
            slot = 2 * m + g % 2
            planes = 4 if m == 1 or g < 2 else 3
            nc.vector.tensor_reduce(
                out=mx[pair][:, slot * P : (slot + 1) * P],
                in_=c1[(g, m)][:, 0 : planes * P].rearrange("p (q n) -> p n q", q=planes),
                axis=AXIS.X,
                op=ALU.max,
            )

        def pool_finish(pair, slabs):
            image = pair // 2
            half = pair % 2
            here = slice(half * 256, (half + 1) * 256)
            if half == 0:
                o1[image] = opool.tile([P, 2, 512], F32, name="o1", bufs=4)
            for m in slabs:
                cols = slice(m * 256, (m + 1) * 256)
                if m == 0 and pair > 0:
                    nc.vector.scalar_tensor_tensor(
                        out=o1[image][:, m, here], in0=mx[pair][:, cols], scalar=0.0, in1=sums[pair][:, cols], op0=ALU.max, op1=ALU.add
                    )
                else:
                    nc.vector.scalar_tensor_tensor(
                        out=o1[image][:, m, here], in0=sums[pair][:, cols], scalar=0.25, in1=mx[pair][:, cols], op0=ALU.mult, op1=ALU.add
                    )
            part = slice(slabs[0], slabs[-1] + 1)
            c1p_rows = out_0[image].rearrange("(m p) i j -> p m (i j)", p=P)
            if image == 3:
                nc.sync.dma_start(out=c1p_rows[:, part, here], in_=o1[image][:, part, here])
            elif half == 1:
                nc.sync.dma_start(out=c1p_rows, in_=o1[image][:])

        def copy_part(g):
            pair = g // 2
            for m in range(2):
                if g % 2 == 0:
                    o2[(pair, m)] = opool.tile([P, 2 * CHUNK], F32, name="o2", bufs=12)
                dst = o2[(pair, m)][:, (g % 2) * CHUNK : (g % 2 + 1) * CHUNK].rearrange(
                    "p (i a j b) -> p a i j b", i=8, a=2, j=16, b=2
                )
                src = c2[(g, m)][:].rearrange("p (a b i j) -> p a i j b", a=2, b=2, i=8, j=16)
                nc.scalar.copy(out=dst, in_=src)

        def store(g):
            pair = g // 2
            image = g // 4
            half = pair % 2
            c2_rows = out_1[image].rearrange("(m p) h w -> p m (h w)", p=P)
            if pair >= FINE_PAIR:
                first = (g % 4) * CHUNK
                for m in range(2):
                    nc.sync.dma_start(
                        out=c2_rows[:, m, first : first + CHUNK], in_=o2[(pair, m)][:, (g % 2) * CHUNK : (g % 2 + 1) * CHUNK]
                    )
            elif g % 2 == 1:
                for m in range(2):
                    nc.sync.dma_start(out=c2_rows[:, m, half * 1024 : (half + 1) * 1024], in_=o2[(pair, m)][:])

        def dummies(count):
            for n in range(count):
                idle = psum.tile([P, 512], F32, name="idle", tag="c1", bufs=3)
                nc.tensor.matmul(out=idle[:], lhsT=warm[:, 0:P], rhs=warm[:], start=True, stop=True)

        dummies(WARM_UP)
        w_transpose(0)
        w_transpose(1)
        dummies(KEEP_WARM)
        regroup_even_rows(0)
        regroup_odd_rows(0)
        w_copy(0)
        w_copy(1)
        quantise(0)
        w_quantise(0)
        regroup_even_rows(1)
        regroup_odd_rows(1)
        variants()
        w_quantise(1)
        multiply(0)
        for g in range(N_CHUNKS):
            if g == 0:
                pool_max(g, 0)
                pool_max(g, 1)
                variants_quantise()
            if g + 1 < N_CHUNKS:
                quantise(g + 1)
                multiply(g + 1)
            if g + 2 < N_CHUNKS:
                regroup_even_rows(g + 2)
                regroup_odd_rows(g + 2)
            if g % 2 == 0 and g >= 2:
                pool_finish(g // 2 - 1, (0, 1))
            copy_part(g)
            store(g)
            if g >= 1:
                pool_max(g, 0)
                pool_max(g, 1)
        for m in range(2):
            pool_finish(N_PAIRS - 1, (m,))
